import numpy as np
import ml_dtypes


def mxq(x, axis, fmt="e4m3"):
    dtype, down = {"e4m3": (ml_dtypes.float8_e4m3fn, 7), "e5m2": (ml_dtypes.float8_e5m2, 14)}[fmt]
    v = np.moveaxis(np.asarray(x, np.float32).astype(ml_dtypes.bfloat16).astype(np.float64), axis, -1)
    blocks = v.reshape(v.shape[:-1] + (-1, 32))
    amax = np.abs(blocks).max(-1, keepdims=True)
    byte = np.maximum(np.where(amax > 0, np.frexp(amax)[1] - 1 + 127, 0) - down, 1)
    scale = np.exp2(byte - 127.0)
    codes = (blocks / scale).astype(np.float32).astype(dtype).astype(np.float64)
    return np.moveaxis((codes * scale).reshape(v.shape), -1, axis)


WIDE = False


def mx_kscale(k):
    if not WIDE:
        return np.ones(k)
    levels = np.array([10, -10, 5, -5, 0])
    a = np.random.permutation(np.resize(levels, k // 512 * 4)).reshape(k // 512, 4)
    idx = np.arange(k)
    return np.exp2(a[idx // 512, idx % 128 // 32])


BF16 = ml_dtypes.bfloat16


def bf(x):
    return np.asarray(x, np.float32).astype(BF16)


def f64(x):
    return np.asarray(x).astype(np.float64)


B, N, D, H, DK, P = 4, 2048, 512, 2, 128, 512
E = H * DK


def setup_inputs():
    s = mx_kscale(D)
    return {"Q": bf(np.random.standard_normal((B, N, D)) * s),
            "WQ": bf(np.random.standard_normal((E, D)) * 1.5 / np.sqrt(D) / s)}


def reference(Q, WQ):
    q = mxq(f64(Q), 2, "e4m3") @ mxq(f64(WQ), 1, "e4m3").T
    q = q.reshape(B, N, H, DK).transpose(0, 2, 1, 3)
    g = np.exp(q - q.max(-1, keepdims=True))
    return g / g.sum(-1, keepdims=True)

@@ -1,0 +1,180 @@
+from contextlib import ExitStack
+
+import concourse.mybir as mybir
+from concourse.masks import make_identity
+
+F32 = mybir.dt.float32
+BF16 = mybir.dt.bfloat16
+U32 = mybir.dt.uint32
+U8 = mybir.dt.uint8
+FP8X4 = mybir.dt.float8_e4m3fn_x4
+
+P = 128
+PACK = 4
+HALVES = 2
+TOKENS = 4 * 2048
+BATCH_TOKENS = 2048
+K = 512
+HEADS = 2
+HEAD_DIM = 128
+FEATURES = HEADS * HEAD_DIM
+TILES = 4
+TILES_PER_BANK = 2
+GROUP_TOKENS = TILES * P
+GROUPS = TOKENS // GROUP_TOKENS
+
+FLOPS = 2 * TOKENS * FEATURES * K
+
+
+def tile_multiheadattention_pb_t_kernel(tc, Q, WQ, out):
+    nc = tc.nc
+    with ExitStack() as ctx:
+        const = ctx.enter_context(tc.tile_pool(name="const", bufs=1))
+        rows_pool = ctx.enter_context(tc.tile_pool(name="rows", bufs=GROUPS))
+        operand_pool = ctx.enter_context(tc.tile_pool(name="operand", bufs=3))
+        stats_pool = ctx.enter_context(tc.tile_pool(name="stats", bufs=4))
+        probs_pool = ctx.enter_context(tc.tile_pool(name="probs", bufs=4))
+        flipped_pool = ctx.enter_context(tc.psum_pool(name="flipped", bufs=4))
+        logits_pool = ctx.enter_context(tc.psum_pool(name="logits", bufs=4))
+        ctx.enter_context(tc.manual_schedule())
+
+        w_rows = const.tile([P, HEADS * K], BF16)
+        nc.sync.dma_start(
+            out=w_rows[:].rearrange("p (h k) -> p h k", h=HEADS),
+            in_=WQ.rearrange("(h p) k -> p h k", p=P),
+        )
+        q_groups = Q.flatten_outer_dims().rearrange("(g p t) k -> g p (t k)", p=P, t=TILES)
+        q_rows = []
+        for g in range(GROUPS):
+            rows = rows_pool.tile([P, TILES * K], BF16)
+            nc.sync.dma_start(out=rows[:], in_=q_groups[g])
+            q_rows.append(rows)
+
+        ident = const.tile([P, P], F32)
+        make_identity(nc, ident[:])
+
+        warm = const.tile([P, 1], F32)
+        nc.vector.memset(warm[:], 0.0)
+        nc.scalar.activation(out=warm[:], in_=warm[:], func=mybir.ActivationFunctionType.Exp)
+
+        def regroup(rows, n_tiles, grouped):
+            words = rows[:].bitcast(F32).rearrange("p (j w) -> p j w", j=n_tiles)
+            grouped_words = grouped[:].bitcast(F32).rearrange(
+                "p (j r u) -> p j r u", j=n_tiles, u=HALVES
+            )
+            for first in range(0, n_tiles, TILES_PER_BANK):
+                flipped = flipped_pool.tile([P, TILES_PER_BANK, HALVES, P], F32)
+                for j in range(TILES_PER_BANK):
+                    for u in range(HALVES):
+                        nc.tensor.transpose(
+                            flipped[:, j, u, :],
+                            words[:, first + j, u * P : (u + 1) * P],
+                            ident[:],
+                        )
+                nc.scalar.copy(
+                    out=grouped_words[:, first : first + TILES_PER_BANK, :, :],
+                    in_=flipped[:].rearrange("p j u r -> p j r u"),
+                )
+
+        w_grouped = const.tile([P, FEATURES * PACK], BF16, align_bytes=64)
+        w_codes = const.tile([P, FEATURES], U32, align_bytes=64)
+        w_scales = const.tile([P, FEATURES], U8, align_bytes=64)
+        regroup(w_rows, HEADS, w_grouped)
+        nc.vector.quantize_mx(out=w_codes[:].bitcast(FP8X4), scales=w_scales[:], in_=w_grouped[:])
+
+        grouped_of = {}
+        logits_of = {}
+        neg_max_of = {}
+        sums_of = {}
+        probs_of = {}
+        codes_of = {}
+
+        def stage_regroup(g):
+            grouped = operand_pool.tile([P, GROUP_TOKENS * PACK], BF16, align_bytes=64)
+            regroup(q_rows[g], TILES, grouped)
+            grouped_of[g] = grouped
+
+        def stage_quantise(g):
+            codes = operand_pool.tile([P, GROUP_TOKENS], U32, align_bytes=64)
+            scales = operand_pool.tile([P, GROUP_TOKENS], U8, align_bytes=64)
+            nc.vector.quantize_mx(
+                out=codes[:].bitcast(FP8X4), scales=scales[:], in_=grouped_of[g][:]
+            )
+            codes_of[g] = (codes, scales)
+
+        def stage_project(g):
+            codes, scales = codes_of[g]
+            neg_max = stats_pool.tile([P, TILES * HEADS], F32)
+            banks = []
+            for first in range(0, TILES, TILES_PER_BANK):
+                logits = logits_pool.tile([P, TILES_PER_BANK, FEATURES], F32)
+                for j in range(TILES_PER_BANK):
+                    tokens = slice((first + j) * P, (first + j + 1) * P)
+                    nc.tensor.matmul_mx(
+                        out=logits[:, j, :],
+                        lhsT=codes[:, tokens].bitcast(FP8X4),
+                        lhsT_scale=scales[:, tokens],
+                        rhs=w_codes[:].bitcast(FP8X4),
+                        rhs_scale=w_scales[:],
+                        start=True,
+                        stop=True,
+                    )
+                nc.vector.tensor_reduce(
+                    out=neg_max[:, first * HEADS : (first + TILES_PER_BANK) * HEADS],
+                    in_=logits[:].rearrange("p j (h d) -> p (j h) d", h=HEADS),
+                    axis=mybir.AxisListType.X,
+                    op=mybir.AluOpType.max,
+                    negate=True,
+                )
+                banks.append(logits)
+            logits_of[g] = banks
+            neg_max_of[g] = neg_max
+
+        def stage_exp(g):
+            probs = probs_pool.tile([P, HEADS, TILES, HEAD_DIM], F32)
+            sums = stats_pool.tile([P, TILES * HEADS], F32)
+            for t in range(TILES):
+                logits = logits_of[g][t // TILES_PER_BANK]
+                for h in range(HEADS):
+                    col = t * HEADS + h
+                    nc.scalar.activation(
+                        out=probs[:, h, t, :],
+                        in_=logits[:, t % TILES_PER_BANK, h * HEAD_DIM : (h + 1) * HEAD_DIM],
+                        func=mybir.ActivationFunctionType.Exp,
+                        bias=neg_max_of[g][:, col : col + 1],
+                        accum_out=sums[:, col : col + 1],
+                    )
+            probs_of[g] = probs
+            sums_of[g] = sums
+
+        def stage_normalise(g):
+            probs = probs_of[g]
+            inverse = stats_pool.tile([P, TILES * HEADS], F32)
+            nc.vector.reciprocal(out=inverse[:], in_=sums_of[g][:])
+            for t in range(TILES):
+                for h in range(HEADS):
+                    col = t * HEADS + h
+                    nc.vector.tensor_scalar_mul(
+                        out=probs[:, h, t, :],
+                        in0=probs[:, h, t, :],
+                        scalar1=inverse[:, col : col + 1],
+                    )
+            b, first_token = divmod(g * GROUP_TOKENS, BATCH_TOKENS)
+            nc.sync.dma_start(
+                out=out[b, :, first_token : first_token + GROUP_TOKENS, :].rearrange(
+                    "h (p t) d -> p h (t d)", t=TILES
+                ),
+                in_=probs[:].rearrange("p h t d -> p h (t d)"),
+            )
+
+        for step in range(GROUPS + 3):
+            if step < GROUPS:
+                stage_regroup(step)
+            if 0 <= step - 1 < GROUPS:
+                stage_quantise(step - 1)
+            if 0 <= step - 3 < GROUPS:
+                stage_normalise(step - 3)
+            if 0 <= step - 1 < GROUPS:
+                stage_project(step - 1)
+            if 0 <= step - 2 < GROUPS:
+                stage_exp(step - 2)

@@ -20,8 +20,10 @@ HEAD_DIM = 128
 FEATURES = HEADS * HEAD_DIM
 TILES = 4
 TILES_PER_BANK = 2
+BANKS = TILES // TILES_PER_BANK
 GROUP_TOKENS = TILES * P
 GROUPS = TOKENS // GROUP_TOKENS
+COPY_CYCLE = 6
 
 FLOPS = 2 * TOKENS * FEATURES * K
 
@@ -34,8 +36,8 @@ def tile_multiheadattention_pb_t_kernel(tc, Q, WQ, out):
         operand_pool = ctx.enter_context(tc.tile_pool(name="operand", bufs=3))
         stats_pool = ctx.enter_context(tc.tile_pool(name="stats", bufs=4))
         probs_pool = ctx.enter_context(tc.tile_pool(name="probs", bufs=4))
-        flipped_pool = ctx.enter_context(tc.psum_pool(name="flipped", bufs=4))
-        logits_pool = ctx.enter_context(tc.psum_pool(name="logits", bufs=4))
+        flipped_pool = ctx.enter_context(tc.psum_pool(name="flipped", bufs=BANKS))
+        logits_pool = ctx.enter_context(tc.psum_pool(name="logits", bufs=3 * BANKS))
         ctx.enter_context(tc.manual_schedule())
 
         w_rows = const.tile([P, HEADS * K], BF16)
@@ -57,11 +59,9 @@ def tile_multiheadattention_pb_t_kernel(tc, Q, WQ, out):
         nc.vector.memset(warm[:], 0.0)
         nc.scalar.activation(out=warm[:], in_=warm[:], func=mybir.ActivationFunctionType.Exp)
 
-        def regroup(rows, n_tiles, grouped):
+        def flip(rows, n_tiles):
             words = rows[:].bitcast(F32).rearrange("p (j w) -> p j w", j=n_tiles)
-            grouped_words = grouped[:].bitcast(F32).rearrange(
-                "p (j r u) -> p j r u", j=n_tiles, u=HALVES
-            )
+            banks = []
             for first in range(0, n_tiles, TILES_PER_BANK):
                 flipped = flipped_pool.tile([P, TILES_PER_BANK, HALVES, P], F32)
                 for j in range(TILES_PER_BANK):
@@ -71,40 +71,48 @@ def tile_multiheadattention_pb_t_kernel(tc, Q, WQ, out):
                             words[:, first + j, u * P : (u + 1) * P],
                             ident[:],
                         )
-                nc.scalar.copy(
-                    out=grouped_words[:, first : first + TILES_PER_BANK, :, :],
-                    in_=flipped[:].rearrange("p j u r -> p j r u"),
-                )
+                banks.append(flipped)
+            return banks
+
+        def lay_side_by_side(banks, grouped, first_bank):
+            grouped_words = grouped[:].bitcast(F32).rearrange(
+                "p (i j r u) -> p i j r u", i=len(banks), j=TILES_PER_BANK, u=HALVES
+            )
+            for i, flipped in enumerate(banks):
+                if (first_bank + i) % COPY_CYCLE == 1:
+                    copy_out = nc.vector.tensor_copy
+                else:
+                    copy_out = nc.scalar.copy
+                copy_out(out=grouped_words[:, i], in_=flipped[:].rearrange("p j u r -> p j r u"))
 
         w_grouped = const.tile([P, FEATURES * PACK], BF16, align_bytes=64)
         w_codes = const.tile([P, FEATURES], U32, align_bytes=64)
         w_scales = const.tile([P, FEATURES], U8, align_bytes=64)
-        regroup(w_rows, HEADS, w_grouped)
+        lay_side_by_side(flip(w_rows, HEADS), w_grouped, 0)
         nc.vector.quantize_mx(out=w_codes[:].bitcast(FP8X4), scales=w_scales[:], in_=w_grouped[:])
 
+        flipped_of = {}
         grouped_of = {}
+        codes_of = {}
         logits_of = {}
         neg_max_of = {}
         sums_of = {}
         probs_of = {}
-        codes_of = {}
 
-        def stage_regroup(g):
+        def stage_flip(g):
+            flipped_of[g] = flip(q_rows[g], TILES)
+
+        def stage_copy(g):
             grouped = operand_pool.tile([P, GROUP_TOKENS * PACK], BF16, align_bytes=64)
-            regroup(q_rows[g], TILES, grouped)
+            lay_side_by_side(flipped_of[g], grouped, g * BANKS)
             grouped_of[g] = grouped
 
-        def stage_quantise(g):
+        def stage_project(g):
             codes = operand_pool.tile([P, GROUP_TOKENS], U32, align_bytes=64)
             scales = operand_pool.tile([P, GROUP_TOKENS], U8, align_bytes=64)
             nc.vector.quantize_mx(
                 out=codes[:].bitcast(FP8X4), scales=scales[:], in_=grouped_of[g][:]
             )
-            codes_of[g] = (codes, scales)
-
-        def stage_project(g):
-            codes, scales = codes_of[g]
-            neg_max = stats_pool.tile([P, TILES * HEADS], F32)
             banks = []
             for first in range(0, TILES, TILES_PER_BANK):
                 logits = logits_pool.tile([P, TILES_PER_BANK, FEATURES], F32)
@@ -119,15 +127,20 @@ def tile_multiheadattention_pb_t_kernel(tc, Q, WQ, out):
                         start=True,
                         stop=True,
                     )
+                banks.append(logits)
+            logits_of[g] = banks
+
+        def stage_max(g):
+            neg_max = stats_pool.tile([P, TILES * HEADS], F32)
+            per_bank = TILES_PER_BANK * HEADS
+            for i, logits in enumerate(logits_of[g]):
                 nc.vector.tensor_reduce(
-                    out=neg_max[:, first * HEADS : (first + TILES_PER_BANK) * HEADS],
+                    out=neg_max[:, i * per_bank : (i + 1) * per_bank],
                     in_=logits[:].rearrange("p j (h d) -> p (j h) d", h=HEADS),
                     axis=mybir.AxisListType.X,
                     op=mybir.AluOpType.max,
                     negate=True,
                 )
-                banks.append(logits)
-            logits_of[g] = banks
             neg_max_of[g] = neg_max
 
         def stage_exp(g):
@@ -167,14 +180,14 @@ def tile_multiheadattention_pb_t_kernel(tc, Q, WQ, out):
                 in_=probs[:].rearrange("p h t d -> p h (t d)"),
             )
 
-        for step in range(GROUPS + 3):
-            if step < GROUPS:
-                stage_regroup(step)
-            if 0 <= step - 1 < GROUPS:
-                stage_quantise(step - 1)
-            if 0 <= step - 3 < GROUPS:
-                stage_normalise(step - 3)
-            if 0 <= step - 1 < GROUPS:
-                stage_project(step - 1)
-            if 0 <= step - 2 < GROUPS:
-                stage_exp(step - 2)
+        def run(stage, g):
+            if 0 <= g < GROUPS:
+                stage(g)
+
+        for step in range(GROUPS + 4):
+            run(stage_flip, step)
+            run(stage_project, step - 1)
+            run(stage_max, step - 2)
+            run(stage_copy, step)
+            run(stage_normalise, step - 4)
+            run(stage_exp, step - 3)

@@ -23,7 +23,7 @@ TILES_PER_BANK = 2
 BANKS = TILES // TILES_PER_BANK
 GROUP_TOKENS = TILES * P
 GROUPS = TOKENS // GROUP_TOKENS
-COPY_CYCLE = 6
+COPY_CYCLE = 4
 
 FLOPS = 2 * TOKENS * FEATURES * K
 
@@ -98,6 +98,7 @@ def tile_multiheadattention_pb_t_kernel(tc, Q, WQ, out):
         neg_max_of = {}
         sums_of = {}
         probs_of = {}
+        inverse_of = {}
 
         def stage_flip(g):
             flipped_of[g] = flip(q_rows[g], TILES)
@@ -160,18 +161,27 @@ def tile_multiheadattention_pb_t_kernel(tc, Q, WQ, out):
             probs_of[g] = probs
             sums_of[g] = sums
 
-        def stage_normalise(g):
-            probs = probs_of[g]
+        def stage_invert(g):
             inverse = stats_pool.tile([P, TILES * HEADS], F32)
             nc.vector.reciprocal(out=inverse[:], in_=sums_of[g][:])
+            inverse_of[g] = inverse
+            of_head_1 = inverse[:].rearrange("p (t h) -> p h t", h=HEADS)[:, 1, :]
+            nc.gpsimd.tensor_tensor(
+                out=probs_of[g][:, 1, :, :],
+                in0=probs_of[g][:, 1, :, :],
+                in1=of_head_1.unsqueeze(2).to_broadcast([P, TILES, HEAD_DIM]),
+                op=mybir.AluOpType.mult,
+            )
+
+        def stage_normalise(g):
+            probs = probs_of[g]
             for t in range(TILES):
-                for h in range(HEADS):
-                    col = t * HEADS + h
-                    nc.vector.tensor_scalar_mul(
-                        out=probs[:, h, t, :],
-                        in0=probs[:, h, t, :],
-                        scalar1=inverse[:, col : col + 1],
-                    )
+                col = t * HEADS
+                nc.vector.tensor_scalar_mul(
+                    out=probs[:, 0, t, :],
+                    in0=probs[:, 0, t, :],
+                    scalar1=inverse_of[g][:, col : col + 1],
+                )
             b, first_token = divmod(g * GROUP_TOKENS, BATCH_TOKENS)
             nc.sync.dma_start(
                 out=out[b, :, first_token : first_token + GROUP_TOKENS, :].rearrange(
@@ -187,6 +197,7 @@ def tile_multiheadattention_pb_t_kernel(tc, Q, WQ, out):
         for step in range(GROUPS + 4):
             run(stage_flip, step)
             run(stage_project, step - 1)
+            run(stage_invert, step - 4)
             run(stage_max, step - 2)
             run(stage_copy, step)
             run(stage_normalise, step - 4)

from contextlib import ExitStack

import concourse.mybir as mybir
from concourse.masks import make_identity

F32 = mybir.dt.float32
BF16 = mybir.dt.bfloat16
U32 = mybir.dt.uint32
U8 = mybir.dt.uint8
FP8X4 = mybir.dt.float8_e4m3fn_x4

P = 128
PACK = 4
HALVES = 2
TOKENS = 4 * 2048
BATCH_TOKENS = 2048
K = 512
HEADS = 2
HEAD_DIM = 128
FEATURES = HEADS * HEAD_DIM
TILES = 4
TILES_PER_BANK = 2
BANKS = TILES // TILES_PER_BANK
GROUP_TOKENS = TILES * P
GROUPS = TOKENS // GROUP_TOKENS
COPY_CYCLE = 4

FLOPS = 2 * TOKENS * FEATURES * K


def tile_multiheadattention_pb_t_kernel(tc, Q, WQ, out):
    nc = tc.nc
    with ExitStack() as ctx:
        const = ctx.enter_context(tc.tile_pool(name="const", bufs=1))
        rows_pool = ctx.enter_context(tc.tile_pool(name="rows", bufs=GROUPS))
        operand_pool = ctx.enter_context(tc.tile_pool(name="operand", bufs=3))
        stats_pool = ctx.enter_context(tc.tile_pool(name="stats", bufs=4))
        probs_pool = ctx.enter_context(tc.tile_pool(name="probs", bufs=4))
        flipped_pool = ctx.enter_context(tc.psum_pool(name="flipped", bufs=BANKS))
        logits_pool = ctx.enter_context(tc.psum_pool(name="logits", bufs=3 * BANKS))
        ctx.enter_context(tc.manual_schedule())

        w_rows = const.tile([P, HEADS * K], BF16)
        nc.sync.dma_start(
            out=w_rows[:].rearrange("p (h k) -> p h k", h=HEADS),
            in_=WQ.rearrange("(h p) k -> p h k", p=P),
        )
        q_groups = Q.flatten_outer_dims().rearrange("(g p t) k -> g p (t k)", p=P, t=TILES)
        q_rows = []
        for g in range(GROUPS):
            rows = rows_pool.tile([P, TILES * K], BF16)
            nc.sync.dma_start(out=rows[:], in_=q_groups[g])
            q_rows.append(rows)

        ident = const.tile([P, P], F32)
        make_identity(nc, ident[:])

        warm = const.tile([P, 1], F32)
        nc.vector.memset(warm[:], 0.0)
        nc.scalar.activation(out=warm[:], in_=warm[:], func=mybir.ActivationFunctionType.Exp)

        def flip(rows, n_tiles):
            words = rows[:].bitcast(F32).rearrange("p (j w) -> p j w", j=n_tiles)
            banks = []
            for first in range(0, n_tiles, TILES_PER_BANK):
                flipped = flipped_pool.tile([P, TILES_PER_BANK, HALVES, P], F32)
                for j in range(TILES_PER_BANK):
                    for u in range(HALVES):
                        nc.tensor.transpose(
                            flipped[:, j, u, :],
                            words[:, first + j, u * P : (u + 1) * P],
                            ident[:],
                        )
                banks.append(flipped)
            return banks

        def lay_side_by_side(banks, grouped, first_bank):
            grouped_words = grouped[:].bitcast(F32).rearrange(
                "p (i j r u) -> p i j r u", i=len(banks), j=TILES_PER_BANK, u=HALVES
            )
            for i, flipped in enumerate(banks):
                if (first_bank + i) % COPY_CYCLE == 1:
                    copy_out = nc.vector.tensor_copy
                else:
                    copy_out = nc.scalar.copy
                copy_out(out=grouped_words[:, i], in_=flipped[:].rearrange("p j u r -> p j r u"))

        w_grouped = const.tile([P, FEATURES * PACK], BF16, align_bytes=64)
        w_codes = const.tile([P, FEATURES], U32, align_bytes=64)
        w_scales = const.tile([P, FEATURES], U8, align_bytes=64)
        lay_side_by_side(flip(w_rows, HEADS), w_grouped, 0)
        nc.vector.quantize_mx(out=w_codes[:].bitcast(FP8X4), scales=w_scales[:], in_=w_grouped[:])

        flipped_of = {}
        grouped_of = {}
        codes_of = {}
        logits_of = {}
        neg_max_of = {}
        sums_of = {}
        probs_of = {}
        inverse_of = {}

        def stage_flip(g):
            flipped_of[g] = flip(q_rows[g], TILES)

        def stage_copy(g):
            grouped = operand_pool.tile([P, GROUP_TOKENS * PACK], BF16, align_bytes=64)
            lay_side_by_side(flipped_of[g], grouped, g * BANKS)
            grouped_of[g] = grouped

        def stage_project(g):
            codes = operand_pool.tile([P, GROUP_TOKENS], U32, align_bytes=64)
            scales = operand_pool.tile([P, GROUP_TOKENS], U8, align_bytes=64)
            nc.vector.quantize_mx(
                out=codes[:].bitcast(FP8X4), scales=scales[:], in_=grouped_of[g][:]
            )
            banks = []
            for first in range(0, TILES, TILES_PER_BANK):
                logits = logits_pool.tile([P, TILES_PER_BANK, FEATURES], F32)
                for j in range(TILES_PER_BANK):
                    tokens = slice((first + j) * P, (first + j + 1) * P)
                    nc.tensor.matmul_mx(
                        out=logits[:, j, :],
                        lhsT=codes[:, tokens].bitcast(FP8X4),
                        lhsT_scale=scales[:, tokens],
                        rhs=w_codes[:].bitcast(FP8X4),
                        rhs_scale=w_scales[:],
                        start=True,
                        stop=True,
                    )
                banks.append(logits)
            logits_of[g] = banks

        def stage_max(g):
            neg_max = stats_pool.tile([P, TILES * HEADS], F32)
            per_bank = TILES_PER_BANK * HEADS
            for i, logits in enumerate(logits_of[g]):
                nc.vector.tensor_reduce(
                    out=neg_max[:, i * per_bank : (i + 1) * per_bank],
                    in_=logits[:].rearrange("p j (h d) -> p (j h) d", h=HEADS),
                    axis=mybir.AxisListType.X,
                    op=mybir.AluOpType.max,
                    negate=True,
                )
            neg_max_of[g] = neg_max

        def stage_exp(g):
            probs = probs_pool.tile([P, HEADS, TILES, HEAD_DIM], F32)
            sums = stats_pool.tile([P, TILES * HEADS], F32)
            for t in range(TILES):
                logits = logits_of[g][t // TILES_PER_BANK]
                for h in range(HEADS):
                    col = t * HEADS + h
                    nc.scalar.activation(
                        out=probs[:, h, t, :],
                        in_=logits[:, t % TILES_PER_BANK, h * HEAD_DIM : (h + 1) * HEAD_DIM],
                        func=mybir.ActivationFunctionType.Exp,
                        bias=neg_max_of[g][:, col : col + 1],
                        accum_out=sums[:, col : col + 1],
                    )
            probs_of[g] = probs
            sums_of[g] = sums

        def stage_invert(g):
            inverse = stats_pool.tile([P, TILES * HEADS], F32)
            nc.vector.reciprocal(out=inverse[:], in_=sums_of[g][:])
            inverse_of[g] = inverse
            of_head_1 = inverse[:].rearrange("p (t h) -> p h t", h=HEADS)[:, 1, :]
            nc.gpsimd.tensor_tensor(
                out=probs_of[g][:, 1, :, :],
                in0=probs_of[g][:, 1, :, :],
                in1=of_head_1.unsqueeze(2).to_broadcast([P, TILES, HEAD_DIM]),
                op=mybir.AluOpType.mult,
            )

        def stage_normalise(g):
            probs = probs_of[g]
            for t in range(TILES):
                col = t * HEADS
                nc.vector.tensor_scalar_mul(
                    out=probs[:, 0, t, :],
                    in0=probs[:, 0, t, :],
                    scalar1=inverse_of[g][:, col : col + 1],
                )
            b, first_token = divmod(g * GROUP_TOKENS, BATCH_TOKENS)
            nc.sync.dma_start(
                out=out[b, :, first_token : first_token + GROUP_TOKENS, :].rearrange(
                    "h (p t) d -> p h (t d)", t=TILES
                ),
                in_=probs[:].rearrange("p h t d -> p h (t d)"),
            )

        def run(stage, g):
            if 0 <= g < GROUPS:
                stage(g)

        for step in range(GROUPS + 4):
            run(stage_flip, step)
            run(stage_project, step - 1)
            run(stage_invert, step - 4)
            run(stage_max, step - 2)
            run(stage_copy, step)
            run(stage_normalise, step - 4)
            run(stage_exp, step - 3)
